import numpy as np
import ml_dtypes


def mxq(x, axis, fmt="e4m3"):
    dtype, down = {"e4m3": (ml_dtypes.float8_e4m3fn, 7), "e5m2": (ml_dtypes.float8_e5m2, 14)}[fmt]
    v = np.moveaxis(np.asarray(x, np.float32).astype(ml_dtypes.bfloat16).astype(np.float64), axis, -1)
    blocks = v.reshape(v.shape[:-1] + (-1, 32))
    amax = np.abs(blocks).max(-1, keepdims=True)
    byte = np.maximum(np.where(amax > 0, np.frexp(amax)[1] - 1 + 127, 0) - down, 1)
    scale = np.exp2(byte - 127.0)
    codes = (blocks / scale).astype(np.float32).astype(dtype).astype(np.float64)
    return np.moveaxis((codes * scale).reshape(v.shape), -1, axis)


WIDE = False


def mx_kscale(k):
    if not WIDE:
        return np.ones(k)
    levels = np.array([10, -10, 5, -5, 0])
    if k % 512:
        return np.exp2(np.random.permutation(np.resize(levels, k // 32))).repeat(32)
    a = np.empty((k // 512, 16))
    for p in range(k // 512):
        a[p, :8] = np.random.permutation(np.resize(levels, 8))
        for g in range(8):
            far = levels[np.abs(levels - a[p, g]) >= 10]
            a[p, g + 8] = far[np.random.randint(len(far))]
    return np.exp2(a.ravel()).repeat(32)


BF16 = ml_dtypes.bfloat16


def bf(x):
    return np.asarray(x, np.float32).astype(BF16)


def f64(x):
    return np.asarray(x).astype(np.float64)


B, N, D, DO, H, HID = 12, 128, 512, 512, 8, 2048


def setup_inputs():
    s, t = mx_kscale(D), mx_kscale(D)
    adj = np.random.uniform(size=(N, N))
    adj = adj / adj.sum(-1, keepdims=True)
    return {
        "h_norm": bf(np.random.standard_normal((B, N, D)) * s),
        "o_attn": bf(np.random.standard_normal((B, N, D)) * 0.25 * t),
        "a_gcn": bf(adj + np.random.standard_normal((N, N)) * 0.5 / np.sqrt(N)),
        "w_proj": bf(np.random.standard_normal((D, DO)) * 2.0 / np.sqrt(D) / t[:, None]),
        "b_proj": bf(np.random.standard_normal(DO) * 0.1),
        "gcn_w": bf(np.random.standard_normal((D, DO)) / np.sqrt(D) / s[:, None]),
        "gcn_m": bf(1.0 + 0.1 * np.random.standard_normal(DO)),
    }


def reference(h_norm, o_attn, a_gcn, w_proj, b_proj, gcn_w, gcn_m):
    o = (mxq(f64(o_attn), 2, "e4m3") @ mxq(f64(w_proj), 0, "e4m3")) + f64(b_proj)
    agg = f64(a_gcn) @ f64(h_norm)
    g = (mxq(agg, 2, "e4m3") @ mxq(f64(gcn_w), 0, "e4m3")) * f64(gcn_m)
    return o + g

@@ -1,0 +1,261 @@
+from contextlib import ExitStack
+
+import concourse.mybir as mybir
+from concourse.masks import make_identity
+
+FP8X4 = mybir.dt.float8_e4m3fn_x4
+BF16 = mybir.dt.bfloat16
+F32 = mybir.dt.float32
+U32 = mybir.dt.uint32
+U8 = mybir.dt.uint8
+ADD = mybir.AluOpType.add
+MULT = mybir.AluOpType.mult
+IDENTITY = mybir.ActivationFunctionType.Identity
+
+P = 128
+D = 512
+PACK = 4
+B = 12
+PAIRS = B // 2
+CHUNKS = D // P
+NODE_MAJOR = 8
+FLOPS = 2 * 2 * B * P * D * D + 2 * B * P * P * D
+
+SCALAR_COLS = (160, 128)
+VECTOR_JOINS = (6, 7)
+BANKS = {"front": 4, "proj": 2, "gcn": 2}
+
+
+def tile_gatblock_pa_kernel(tc, h_norm, o_attn, a_gcn, w_proj, b_proj, gcn_w, gcn_m, out):
+    nc = tc.nc
+    with ExitStack() as ctx:
+        sbuf = ctx.enter_context(tc.tile_pool(name="sbuf", bufs=1))
+        psum = ctx.enter_context(tc.psum_pool(name="psum", bufs=1))
+        ctx.enter_context(tc.manual_schedule())
+
+        ident_f = sbuf.tile([P, P], F32, name="ident_f")
+        ident_bf = sbuf.tile([P, P], BF16, name="ident_bf")
+        ones = sbuf.tile([P, P], BF16, name="ones")
+        rows = sbuf.tile([P, 2 * D], BF16, name="rows")
+        spread = sbuf.tile([P, 2 * D], BF16, name="spread")
+        chunk_rows = sbuf.tile([P, P], BF16, name="chunk_rows")
+        per_feature = sbuf.tile([P, 2 * CHUNKS], F32, name="per_feature")
+        warm = sbuf.tile([P, 1], F32, name="warm")
+        a_sb = sbuf.tile([P, P], BF16, name="a_sb")
+        aT_sb = sbuf.tile([P, P], BF16, name="aT_sb")
+        w_dram = (w_proj, gcn_w)
+        w_raw = [sbuf.tile([P, PACK, D], BF16, name="w_raw%d" % w) for w in range(2)]
+        w_grouped = [sbuf.tile([P, D, PACK], BF16, name="w_grouped%d" % w, align_bytes=64) for w in range(2)]
+        w_codes = [sbuf.tile([P, D], U32, name="w_codes%d" % w, align_bytes=64) for w in range(2)]
+        w_scales = [sbuf.tile([P, D], U8, name="w_scales%d" % w, align_bytes=64) for w in range(2)]
+        o_sb = [sbuf.tile([P, 2 * D], BF16, name="o_sb%d" % j) for j in range(PAIRS)]
+        h_sb = [sbuf.tile([P, 2, D], BF16, name="h_sb%d" % j) for j in range(PAIRS)]
+        grouped = [
+            [sbuf.tile([P, 2 * D], BF16, name="grouped%d_%d" % (k, j), align_bytes=64) for j in range(PAIRS)]
+            for k in range(2)
+        ]
+        codes = [
+            [sbuf.tile([P, 2 * P], U32, name="codes%d_%d" % (k, j), align_bytes=64) for j in range(PAIRS)]
+            for k in range(2)
+        ]
+        scales = [
+            [sbuf.tile([P, 2 * P], U8, name="scales%d_%d" % (k, j), align_bytes=64) for j in range(PAIRS)]
+            for k in range(2)
+        ]
+        result = [sbuf.tile([P, D], F32, name="result%d" % b) for b in range(B)]
+        other = [sbuf.tile([P, D], F32, name="other%d" % b) for b in range(B)]
+        scaled_t = {j: sbuf.tile([P, CHUNKS, 2 * P], F32, name="scaled_t%d" % j) for j in range(NODE_MAJOR // 2, PAIRS)}
+        bank = {}
+        taken = {group: 0 for group in BANKS}
+
+        def new_bank(group, shape, dtype, name):
+            tag = "%s%d" % (group, taken[group] % BANKS[group])
+            taken[group] = taken[group] + 1
+            return psum.tile(shape, dtype, name=name, tag=tag)
+
+        def load_weight(w):
+            nc.sync.dma_start(out=w_raw[w][:], in_=w_dram[w].rearrange("(p t) c -> p t c", t=PACK))
+
+        def load_o(j):
+            nc.sync.dma_start(
+                out=o_sb[j][:].rearrange("p (s d) -> p s d", s=2),
+                in_=o_attn[2 * j : 2 * j + 2].rearrange("s n d -> n s d"),
+            )
+
+        def load_h(j):
+            nc.sync.dma_start(out=h_sb[j][:], in_=h_norm[2 * j : 2 * j + 2].rearrange("s n d -> n s d"))
+
+        def store(b):
+            nc.sync.dma_start(out=out[b], in_=result[b][:])
+
+        def regroup(copy, w, c0, c1):
+            copy(
+                out=w_grouped[w][:, c0:c1, :].rearrange("p (c i) t -> p c t i", i=4),
+                in_=w_raw[w][:, :, c0:c1].rearrange("p t (c i) -> p c t i", i=4),
+            )
+
+        def regroup_and_quantise(w):
+            regroup(nc.scalar.copy, w, 0, SCALAR_COLS[w])
+            regroup(nc.vector.tensor_copy, w, SCALAR_COLS[w], D)
+            nc.vector.quantize_mx(
+                out=w_codes[w][:].bitcast(FP8X4),
+                scales=w_scales[w][:],
+                in_=w_grouped[w][:].rearrange("p c t -> p (c t)"),
+            )
+
+        def transpose_o(j):
+            o_t = new_bank("front", [P, 2, 2, P], F32, "o_t%d" % j)
+            words = o_sb[j][:].bitcast(F32)
+            for s in range(2):
+                for u in range(2):
+                    c0 = 2 * P * s
+                    nc.tensor.transpose(o_t[:, s, u, :], words[:, c0 + u : c0 + 2 * P : 2], ident_f[:])
+            nc.scalar.copy(
+                out=grouped[0][j][:].bitcast(F32).rearrange("p (s i u) -> p s i u", s=2, u=2),
+                in_=o_t[:].rearrange("p s u i -> p s i u"),
+            )
+
+        def aggregate(j):
+            agg_t = [new_bank("front", [P, PACK, P], F32, "agg_t%d" % (2 * j + s)) for s in range(2)]
+            for s in range(2):
+                for t in range(PACK):
+                    nc.tensor.matmul(
+                        agg_t[s][:, t, :], lhsT=h_sb[j][:, s, t:D:PACK], rhs=aT_sb[:], start=True, stop=True
+                    )
+            for s in range(2):
+                nc.scalar.copy(
+                    out=grouped[1][j][:, D * s : D * s + D].rearrange("p (i t) -> p i t", t=PACK),
+                    in_=agg_t[s][:].rearrange("p t i -> p i t"),
+                )
+
+        def quantise(branch, j):
+            nc.vector.quantize_mx(
+                out=codes[branch][j][:].bitcast(FP8X4), scales=scales[branch][j][:], in_=grouped[branch][j][:]
+            )
+
+        def product(branch, b, group):
+            j, cols = b // 2, slice(P * (b % 2), P * (b % 2) + P)
+            acc = new_bank(group, [P, D], F32, "acc%d_%d" % (branch, b))
+            nc.tensor.matmul_mx(
+                out=acc[:],
+                lhsT=codes[branch][j][:, cols].bitcast(FP8X4),
+                lhsT_scale=scales[branch][j][:, cols],
+                rhs=w_codes[branch][:].bitcast(FP8X4),
+                rhs_scale=w_scales[branch][:],
+                start=True,
+                stop=True,
+            )
+            bank[branch, b] = acc
+
+        def add_bias(b):
+            product(0, b, "proj")
+            nc.vector.tensor_tensor(out=result[b][:], in0=bank[0, b][:], in1=spread[:, 0:D], op=ADD)
+
+        def apply_gain(b):
+            product(1, b, "gcn")
+            nc.vector.tensor_tensor(out=other[b][:], in0=bank[1, b][:], in1=spread[:, D : 2 * D], op=MULT)
+
+        def join_and_store(engine, b):
+            engine.tensor_tensor(out=result[b][:], in0=result[b][:], in1=other[b][:], op=ADD)
+            store(b)
+
+        def gcn_feature_major(j):
+            halves = [new_bank("front", [P, 2, 2 * P], F32, "g_t%d_%d" % (j, half)) for half in range(2)]
+            for c in range(CHUNKS):
+                nc.tensor.matmul_mx(
+                    out=halves[c // 2][:, c % 2, :],
+                    lhsT=w_codes[1][:, P * c : P * c + P].bitcast(FP8X4),
+                    lhsT_scale=w_scales[1][:, P * c : P * c + P],
+                    rhs=codes[1][j][:].bitcast(FP8X4),
+                    rhs_scale=scales[1][j][:],
+                    start=True,
+                    stop=True,
+                )
+            for c in range(CHUNKS):
+                nc.scalar.activation(
+                    out=scaled_t[j][:, c, :],
+                    in_=halves[c // 2][:, c % 2, :],
+                    func=IDENTITY,
+                    bias=per_feature[:, c : c + 1],
+                    scale=per_feature[:, CHUNKS + c : CHUNKS + c + 1],
+                )
+
+        def projection_out(j):
+            for b in (2 * j, 2 * j + 1):
+                product(0, b, "front")
+            for b in (2 * j, 2 * j + 1):
+                nc.scalar.copy(out=other[b][:], in_=bank[0, b][:])
+
+        def turn_back_join_store(b):
+            back = new_bank("front", [P, D], F32, "back%d" % b)
+            cols = slice(P * (b % 2), P * (b % 2) + P)
+            for c in range(CHUNKS):
+                nc.tensor.transpose(back[:, P * c : P * c + P], scaled_t[b // 2][:, c, cols], ident_f[:])
+            nc.vector.tensor_tensor(out=result[b][:], in0=back[:], in1=other[b][:], op=ADD)
+            store(b)
+
+        nc.vector.memset(rows[:], 0.0)
+        nc.vector.memset(ones[:], 1.0)
+        nc.vector.memset(chunk_rows[:], 0.0)
+        make_identity(nc, ident_f[:])
+        make_identity(nc, ident_bf[:])
+
+        load_weight(0)
+        nc.scalar.dma_start(out=a_sb[:], in_=a_gcn)
+        load_o(0)
+        load_weight(1)
+        load_h(0)
+        load_o(1)
+        nc.scalar.dma_start(out=rows[0:1, 0:D], in_=b_proj.rearrange("(o n) -> o n", o=1))
+        nc.scalar.dma_start(out=rows[0:1, D : 2 * D], in_=gcn_m.rearrange("(o n) -> o n", o=1))
+        nc.scalar.activation(out=warm[:], in_=ident_f[:, 0:1], func=IDENTITY)
+        load_h(1)
+        for j in range(2, PAIRS):
+            load_o(j)
+            load_h(j)
+        nc.sync.dma_start(out=chunk_rows[0:CHUNKS, :], in_=b_proj.rearrange("(c p) -> c p", p=P))
+        nc.sync.dma_start(out=chunk_rows[CHUNKS : 2 * CHUNKS, :], in_=gcn_m.rearrange("(c p) -> c p", p=P))
+
+        regroup_and_quantise(0)
+        transpose_o(0)
+        a_t = new_bank("front", [P, P], BF16, "a_t")
+        nc.tensor.transpose(a_t[:], a_sb[:], ident_bf[:])
+        nc.scalar.copy(out=aT_sb[:], in_=a_t[:])
+        spread_ps = new_bank("gcn", [P, 2 * D], BF16, "spread_ps")
+        for half in range(2):
+            cols = slice(D * half, D * half + D)
+            nc.tensor.matmul(spread_ps[:, cols], lhsT=ones[:], rhs=rows[:, cols], start=True, stop=True)
+        nc.scalar.copy(out=spread[:], in_=spread_ps[:])
+        quantise(0, 0)
+        regroup_and_quantise(1)
+
+        for t in range(PAIRS):
+            aggregate(t)
+            add_bias(t)
+            if t + 1 < PAIRS:
+                transpose_o(t + 1)
+            if t >= 1:
+                apply_gain(t - 1)
+                join_and_store(nc.gpsimd, t - 1)
+            if t == PAIRS - 2:
+                chunk_cols = new_bank("front", [P, P], BF16, "chunk_cols")
+                nc.tensor.transpose(chunk_cols[:], chunk_rows[:], ident_bf[:])
+                nc.scalar.copy(out=per_feature[:], in_=chunk_cols[:, 0 : 2 * CHUNKS])
+            quantise(1, t)
+            if t + 1 < PAIRS:
+                quantise(0, t + 1)
+
+        gcn_feature_major(4)
+        add_bias(6)
+        apply_gain(5)
+        join_and_store(nc.gpsimd, 5)
+        projection_out(4)
+        add_bias(7)
+        apply_gain(6)
+        gcn_feature_major(5)
+        apply_gain(7)
+        projection_out(5)
+        for b in VECTOR_JOINS:
+            join_and_store(nc.vector, b)
+        for b in range(NODE_MAJOR, B):
+            turn_back_join_store(b)

@@ -21,9 +21,8 @@ CHUNKS = D // P
 NODE_MAJOR = 8
 FLOPS = 2 * 2 * B * P * D * D + 2 * B * P * P * D
 
-SCALAR_COLS = (160, 128)
-VECTOR_JOINS = (6, 7)
-BANKS = {"front": 4, "proj": 2, "gcn": 2}
+SCALAR_COLS = 128
+BANKS = {"front": 4, "product": 4}
 
 
 def tile_gatblock_pa_kernel(tc, h_norm, o_attn, a_gcn, w_proj, b_proj, gcn_w, gcn_m, out):
@@ -50,18 +49,9 @@ def tile_gatblock_pa_kernel(tc, h_norm, o_attn, a_gcn, w_proj, b_proj, gcn_w, gc
         w_scales = [sbuf.tile([P, D], U8, name="w_scales%d" % w, align_bytes=64) for w in range(2)]
         o_sb = [sbuf.tile([P, 2 * D], BF16, name="o_sb%d" % j) for j in range(PAIRS)]
         h_sb = [sbuf.tile([P, 2, D], BF16, name="h_sb%d" % j) for j in range(PAIRS)]
-        grouped = [
-            [sbuf.tile([P, 2 * D], BF16, name="grouped%d_%d" % (k, j), align_bytes=64) for j in range(PAIRS)]
-            for k in range(2)
-        ]
-        codes = [
-            [sbuf.tile([P, 2 * P], U32, name="codes%d_%d" % (k, j), align_bytes=64) for j in range(PAIRS)]
-            for k in range(2)
-        ]
-        scales = [
-            [sbuf.tile([P, 2 * P], U8, name="scales%d_%d" % (k, j), align_bytes=64) for j in range(PAIRS)]
-            for k in range(2)
-        ]
+        grouped = [sbuf.tile([P, 4 * D], BF16, name="grouped%d" % j, align_bytes=64) for j in range(PAIRS)]
+        codes = [sbuf.tile([P, 4 * P], U32, name="codes%d" % j, align_bytes=64) for j in range(PAIRS)]
+        scales = [sbuf.tile([P, 4 * P], U8, name="scales%d" % j, align_bytes=64) for j in range(PAIRS)]
         result = [sbuf.tile([P, D], F32, name="result%d" % b) for b in range(B)]
         other = [sbuf.tile([P, D], F32, name="other%d" % b) for b in range(B)]
         scaled_t = {j: sbuf.tile([P, CHUNKS, 2 * P], F32, name="scaled_t%d" % j) for j in range(NODE_MAJOR // 2, PAIRS)}
@@ -94,13 +84,26 @@ def tile_gatblock_pa_kernel(tc, h_norm, o_attn, a_gcn, w_proj, b_proj, gcn_w, gc
                 in_=w_raw[w][:, :, c0:c1].rearrange("p t (c i) -> p c t i", i=4),
             )
 
-        def regroup_and_quantise(w):
-            regroup(nc.scalar.copy, w, 0, SCALAR_COLS[w])
-            regroup(nc.vector.tensor_copy, w, SCALAR_COLS[w], D)
+        def quantise_weight(w):
             nc.vector.quantize_mx(
                 out=w_codes[w][:].bitcast(FP8X4),
                 scales=w_scales[w][:],
                 in_=w_grouped[w][:].rearrange("p c t -> p (c t)"),
+            )
+
+        def aggregate(j):
+            agg_t = new_bank("front", [P, 2, PACK, P], BF16, "agg_t%d" % j)
+            for s in range(2):
+                for t in range(PACK):
+                    nc.tensor.matmul(
+                        agg_t[:, s, t, :], lhsT=h_sb[j][:, s, t:D:PACK], rhs=aT_sb[:], start=True, stop=True
+                    )
+            bank["agg", j] = agg_t
+
+        def take_agg(j):
+            nc.scalar.copy(
+                out=grouped[j][:, 2 * D : 4 * D].rearrange("p (s i t) -> p s i t", s=2, t=PACK),
+                in_=bank["agg", j][:].rearrange("p s t i -> p s i t"),
             )
 
         def transpose_o(j):
@@ -110,36 +113,30 @@ def tile_gatblock_pa_kernel(tc, h_norm, o_attn, a_gcn, w_proj, b_proj, gcn_w, gc
                 for u in range(2):
                     c0 = 2 * P * s
                     nc.tensor.transpose(o_t[:, s, u, :], words[:, c0 + u : c0 + 2 * P : 2], ident_f[:])
+            bank["o", j] = o_t
+
+        def take_o(j):
             nc.scalar.copy(
-                out=grouped[0][j][:].bitcast(F32).rearrange("p (s i u) -> p s i u", s=2, u=2),
-                in_=o_t[:].rearrange("p s u i -> p s i u"),
+                out=grouped[j][:, 0 : 2 * D].bitcast(F32).rearrange("p (s i u) -> p s i u", s=2, u=2),
+                in_=bank["o", j][:].rearrange("p s u i -> p s i u"),
             )
 
-        def aggregate(j):
-            agg_t = [new_bank("front", [P, PACK, P], F32, "agg_t%d" % (2 * j + s)) for s in range(2)]
-            for s in range(2):
-                for t in range(PACK):
-                    nc.tensor.matmul(
-                        agg_t[s][:, t, :], lhsT=h_sb[j][:, s, t:D:PACK], rhs=aT_sb[:], start=True, stop=True
-                    )
-            for s in range(2):
-                nc.scalar.copy(
-                    out=grouped[1][j][:, D * s : D * s + D].rearrange("p (i t) -> p i t", t=PACK),
-                    in_=agg_t[s][:].rearrange("p t i -> p i t"),
-                )
+        def front_end(j):
+            aggregate(j)
+            take_agg(j)
+            transpose_o(j)
+            take_o(j)
 
-        def quantise(branch, j):
-            nc.vector.quantize_mx(
-                out=codes[branch][j][:].bitcast(FP8X4), scales=scales[branch][j][:], in_=grouped[branch][j][:]
-            )
+        def quantise(j):
+            nc.vector.quantize_mx(out=codes[j][:].bitcast(FP8X4), scales=scales[j][:], in_=grouped[j][:])
 
-        def product(branch, b, group):
-            j, cols = b // 2, slice(P * (b % 2), P * (b % 2) + P)
-            acc = new_bank(group, [P, D], F32, "acc%d_%d" % (branch, b))
+        def product(branch, b):
+            j, c0 = b // 2, P * (2 * branch + b % 2)
+            acc = new_bank("product", [P, D], F32, "acc%d_%d" % (branch, b))
             nc.tensor.matmul_mx(
                 out=acc[:],
-                lhsT=codes[branch][j][:, cols].bitcast(FP8X4),
-                lhsT_scale=scales[branch][j][:, cols],
+                lhsT=codes[j][:, c0 : c0 + P].bitcast(FP8X4),
+                lhsT_scale=scales[j][:, c0 : c0 + P],
                 rhs=w_codes[branch][:].bitcast(FP8X4),
                 rhs_scale=w_scales[branch][:],
                 start=True,
@@ -148,15 +145,15 @@ def tile_gatblock_pa_kernel(tc, h_norm, o_attn, a_gcn, w_proj, b_proj, gcn_w, gc
             bank[branch, b] = acc
 
         def add_bias(b):
-            product(0, b, "proj")
+            product(0, b)
             nc.vector.tensor_tensor(out=result[b][:], in0=bank[0, b][:], in1=spread[:, 0:D], op=ADD)
 
         def apply_gain(b):
-            product(1, b, "gcn")
+            product(1, b)
             nc.vector.tensor_tensor(out=other[b][:], in0=bank[1, b][:], in1=spread[:, D : 2 * D], op=MULT)
 
-        def join_and_store(engine, b):
-            engine.tensor_tensor(out=result[b][:], in0=result[b][:], in1=other[b][:], op=ADD)
+        def join_and_store(b):
+            nc.gpsimd.tensor_tensor(out=result[b][:], in0=result[b][:], in1=other[b][:], op=ADD)
             store(b)
 
         def gcn_feature_major(j):
@@ -166,8 +163,8 @@ def tile_gatblock_pa_kernel(tc, h_norm, o_attn, a_gcn, w_proj, b_proj, gcn_w, gc
                     out=halves[c // 2][:, c % 2, :],
                     lhsT=w_codes[1][:, P * c : P * c + P].bitcast(FP8X4),
                     lhsT_scale=w_scales[1][:, P * c : P * c + P],
-                    rhs=codes[1][j][:].bitcast(FP8X4),
-                    rhs_scale=scales[1][j][:],
+                    rhs=codes[j][:, 2 * P : 4 * P].bitcast(FP8X4),
+                    rhs_scale=scales[j][:, 2 * P : 4 * P],
                     start=True,
                     stop=True,
                 )
@@ -180,11 +177,9 @@ def tile_gatblock_pa_kernel(tc, h_norm, o_attn, a_gcn, w_proj, b_proj, gcn_w, gc
                     scale=per_feature[:, CHUNKS + c : CHUNKS + c + 1],
                 )
 
-        def projection_out(j):
-            for b in (2 * j, 2 * j + 1):
-                product(0, b, "front")
-            for b in (2 * j, 2 * j + 1):
-                nc.scalar.copy(out=other[b][:], in_=bank[0, b][:])
+        def projection_out(b):
+            product(0, b)
+            nc.scalar.copy(out=other[b][:], in_=bank[0, b][:])
 
         def turn_back_join_store(b):
             back = new_bank("front", [P, D], F32, "back%d" % b)
@@ -194,68 +189,84 @@ def tile_gatblock_pa_kernel(tc, h_norm, o_attn, a_gcn, w_proj, b_proj, gcn_w, gc
             nc.vector.tensor_tensor(out=result[b][:], in0=back[:], in1=other[b][:], op=ADD)
             store(b)
 
-        nc.vector.memset(rows[:], 0.0)
-        nc.vector.memset(ones[:], 1.0)
-        nc.vector.memset(chunk_rows[:], 0.0)
-        make_identity(nc, ident_f[:])
-        make_identity(nc, ident_bf[:])
-
-        load_weight(0)
         nc.scalar.dma_start(out=a_sb[:], in_=a_gcn)
-        load_o(0)
-        load_weight(1)
         load_h(0)
-        load_o(1)
+        load_weight(0)
+        nc.vector.memset(rows[:], 0.0)
         nc.scalar.dma_start(out=rows[0:1, 0:D], in_=b_proj.rearrange("(o n) -> o n", o=1))
         nc.scalar.dma_start(out=rows[0:1, D : 2 * D], in_=gcn_m.rearrange("(o n) -> o n", o=1))
+        load_o(0)
+        nc.vector.memset(ones[:], 1.0)
+        nc.vector.memset(chunk_rows[:], 0.0)
+        make_identity(nc, ident_bf[:])
+        make_identity(nc, ident_f[:])
         nc.scalar.activation(out=warm[:], in_=ident_f[:, 0:1], func=IDENTITY)
         load_h(1)
+        load_o(1)
+        load_weight(1)
         for j in range(2, PAIRS):
-            load_o(j)
             load_h(j)
+            load_o(j)
         nc.sync.dma_start(out=chunk_rows[0:CHUNKS, :], in_=b_proj.rearrange("(c p) -> c p", p=P))
         nc.sync.dma_start(out=chunk_rows[CHUNKS : 2 * CHUNKS, :], in_=gcn_m.rearrange("(c p) -> c p", p=P))
 
-        regroup_and_quantise(0)
-        transpose_o(0)
         a_t = new_bank("front", [P, P], BF16, "a_t")
         nc.tensor.transpose(a_t[:], a_sb[:], ident_bf[:])
         nc.scalar.copy(out=aT_sb[:], in_=a_t[:])
-        spread_ps = new_bank("gcn", [P, 2 * D], BF16, "spread_ps")
+        aggregate(0)
+        take_agg(0)
+        regroup(nc.vector.tensor_copy, 0, 0, D)
+        quantise_weight(0)
+        transpose_o(0)
+        take_o(0)
+        aggregate(1)
+        spread_ps = new_bank("product", [P, 2 * D], BF16, "spread_ps")
         for half in range(2):
             cols = slice(D * half, D * half + D)
             nc.tensor.matmul(spread_ps[:, cols], lhsT=ones[:], rhs=rows[:, cols], start=True, stop=True)
         nc.scalar.copy(out=spread[:], in_=spread_ps[:])
-        quantise(0, 0)
-        regroup_and_quantise(1)
+        transpose_o(1)
+        take_o(1)
+        quantise(0)
+        regroup(nc.vector.tensor_copy, 1, SCALAR_COLS, D)
+        regroup(nc.scalar.copy, 1, 0, SCALAR_COLS)
+        add_bias(0)
+        take_agg(1)
+        quantise_weight(1)
+        add_bias(1)
+        aggregate(2)
+        take_agg(2)
+        transpose_o(2)
+        quantise(1)
+        take_o(2)
+        for b in (0, 1):
+            apply_gain(b)
+            join_and_store(b)
 
-        for t in range(PAIRS):
-            aggregate(t)
-            add_bias(t)
-            if t + 1 < PAIRS:
-                transpose_o(t + 1)
-            if t >= 1:
-                apply_gain(t - 1)
-                join_and_store(nc.gpsimd, t - 1)
-            if t == PAIRS - 2:
-                chunk_cols = new_bank("front", [P, P], BF16, "chunk_cols")
-                nc.tensor.transpose(chunk_cols[:], chunk_rows[:], ident_bf[:])
-                nc.scalar.copy(out=per_feature[:], in_=chunk_cols[:, 0 : 2 * CHUNKS])
-            quantise(1, t)
-            if t + 1 < PAIRS:
-                quantise(0, t + 1)
+        def finish(b):
+            add_bias(b)
+            apply_gain(b)
+            join_and_store(b)
 
+        for t in range(2, PAIRS - 1):
+            front_end(t + 1)
+            quantise(t)
+            finish(t)
+
+        chunk_cols = new_bank("front", [P, P], BF16, "chunk_cols")
+        nc.tensor.transpose(chunk_cols[:], chunk_rows[:], ident_bf[:])
+        nc.scalar.copy(out=per_feature[:], in_=chunk_cols[:, 0 : 2 * CHUNKS])
         gcn_feature_major(4)
-        add_bias(6)
+        quantise(5)
+        projection_out(8)
+        add_bias(5)
+        projection_out(9)
         apply_gain(5)
-        join_and_store(nc.gpsimd, 5)
-        projection_out(4)
-        add_bias(7)
-        apply_gain(6)
+        join_and_store(5)
         gcn_feature_major(5)
-        apply_gain(7)
-        projection_out(5)
-        for b in VECTOR_JOINS:
-            join_and_store(nc.vector, b)
+        finish(6)
+        projection_out(10)
+        projection_out(11)
+        finish(7)
         for b in range(NODE_MAJOR, B):
             turn_back_join_store(b)

@@ -35,6 +35,7 @@ def tile_gatblock_pa_kernel(tc, h_norm, o_attn, a_gcn, w_proj, b_proj, gcn_w, gc
         ident_f = sbuf.tile([P, P], F32, name="ident_f")
         ident_bf = sbuf.tile([P, P], BF16, name="ident_bf")
         ones = sbuf.tile([P, P], BF16, name="ones")
+        zeros = sbuf.tile([P, D], BF16, name="zeros")
         rows = sbuf.tile([P, 2 * D], BF16, name="rows")
         spread = sbuf.tile([P, 2 * D], BF16, name="spread")
         chunk_rows = sbuf.tile([P, P], BF16, name="chunk_rows")
@@ -192,6 +193,10 @@ def tile_gatblock_pa_kernel(tc, h_norm, o_attn, a_gcn, w_proj, b_proj, gcn_w, gc
         nc.scalar.dma_start(out=a_sb[:], in_=a_gcn)
         load_h(0)
         load_weight(0)
+        nc.gpsimd.memset(zeros[:].bitcast(U32), 0)
+        idle_ps = new_bank("front", [P, D], F32, "idle_ps")
+        for turn in range(4):
+            nc.tensor.matmul(idle_ps[:], lhsT=zeros[:, 0:P], rhs=zeros[:], start=True, stop=True)
         nc.vector.memset(rows[:], 0.0)
         nc.scalar.dma_start(out=rows[0:1, 0:D], in_=b_proj.rearrange("(o n) -> o n", o=1))
         nc.scalar.dma_start(out=rows[0:1, D : 2 * D], in_=gcn_m.rearrange("(o n) -> o n", o=1))

@@ -76,8 +76,8 @@ def tile_gatblock_pa_kernel(tc, h_norm, o_attn, a_gcn, w_proj, b_proj, gcn_w, gc
         def load_h(j):
             nc.sync.dma_start(out=h_sb[j][:], in_=h_norm[2 * j : 2 * j + 2].rearrange("s n d -> n s d"))
 
-        def store(b):
-            nc.sync.dma_start(out=out[b], in_=result[b][:])
+        def store(b, queue=nc.sync):
+            queue.dma_start(out=out[b], in_=result[b][:])
 
         def regroup(copy, w, c0, c1):
             copy(
@@ -188,7 +188,7 @@ def tile_gatblock_pa_kernel(tc, h_norm, o_attn, a_gcn, w_proj, b_proj, gcn_w, gc
             for c in range(CHUNKS):
                 nc.tensor.transpose(back[:, P * c : P * c + P], scaled_t[b // 2][:, c, cols], ident_f[:])
             nc.vector.tensor_tensor(out=result[b][:], in0=back[:], in1=other[b][:], op=ADD)
-            store(b)
+            store(b, nc.scalar)
 
         nc.scalar.dma_start(out=a_sb[:], in_=a_gcn)
         load_h(0)

@@ -22,6 +22,7 @@ NODE_MAJOR = 8
 FLOPS = 2 * 2 * B * P * D * D + 2 * B * P * P * D
 
 SCALAR_COLS = 128
+IDLE_MATMULS = 4
 BANKS = {"front": 4, "product": 4}
 
 
@@ -34,12 +35,13 @@ def tile_gatblock_pa_kernel(tc, h_norm, o_attn, a_gcn, w_proj, b_proj, gcn_w, gc
 
         ident_f = sbuf.tile([P, P], F32, name="ident_f")
         ident_bf = sbuf.tile([P, P], BF16, name="ident_bf")
-        ones = sbuf.tile([P, P], BF16, name="ones")
         zeros = sbuf.tile([P, D], BF16, name="zeros")
+        ones = sbuf.tile([P, P], BF16, name="ones")
         rows = sbuf.tile([P, 2 * D], BF16, name="rows")
         spread = sbuf.tile([P, 2 * D], BF16, name="spread")
         chunk_rows = sbuf.tile([P, P], BF16, name="chunk_rows")
         per_feature = sbuf.tile([P, 2 * CHUNKS], F32, name="per_feature")
+        zero = sbuf.tile([P, 1], F32, name="zero")
         warm = sbuf.tile([P, 1], F32, name="warm")
         a_sb = sbuf.tile([P, P], BF16, name="a_sb")
         aT_sb = sbuf.tile([P, P], BF16, name="aT_sb")
@@ -67,17 +69,14 @@ def tile_gatblock_pa_kernel(tc, h_norm, o_attn, a_gcn, w_proj, b_proj, gcn_w, gc
         def load_weight(w):
             nc.sync.dma_start(out=w_raw[w][:], in_=w_dram[w].rearrange("(p t) c -> p t c", t=PACK))
 
+        def load_h(j):
+            nc.sync.dma_start(out=h_sb[j][:], in_=h_norm[2 * j : 2 * j + 2].rearrange("s n d -> n s d"))
+
         def load_o(j):
             nc.sync.dma_start(
                 out=o_sb[j][:].rearrange("p (s d) -> p s d", s=2),
                 in_=o_attn[2 * j : 2 * j + 2].rearrange("s n d -> n s d"),
             )
-
-        def load_h(j):
-            nc.sync.dma_start(out=h_sb[j][:], in_=h_norm[2 * j : 2 * j + 2].rearrange("s n d -> n s d"))
-
-        def store(b, queue=nc.sync):
-            queue.dma_start(out=out[b], in_=result[b][:])
 
         def regroup(copy, w, c0, c1):
             copy(
@@ -92,21 +91,6 @@ def tile_gatblock_pa_kernel(tc, h_norm, o_attn, a_gcn, w_proj, b_proj, gcn_w, gc
                 in_=w_grouped[w][:].rearrange("p c t -> p (c t)"),
             )
 
-        def aggregate(j):
-            agg_t = new_bank("front", [P, 2, PACK, P], BF16, "agg_t%d" % j)
-            for s in range(2):
-                for t in range(PACK):
-                    nc.tensor.matmul(
-                        agg_t[:, s, t, :], lhsT=h_sb[j][:, s, t:D:PACK], rhs=aT_sb[:], start=True, stop=True
-                    )
-            bank["agg", j] = agg_t
-
-        def take_agg(j):
-            nc.scalar.copy(
-                out=grouped[j][:, 2 * D : 4 * D].rearrange("p (s i t) -> p s i t", s=2, t=PACK),
-                in_=bank["agg", j][:].rearrange("p s t i -> p s i t"),
-            )
-
         def transpose_o(j):
             o_t = new_bank("front", [P, 2, 2, P], F32, "o_t%d" % j)
             words = o_sb[j][:].bitcast(F32)
@@ -114,19 +98,28 @@ def tile_gatblock_pa_kernel(tc, h_norm, o_attn, a_gcn, w_proj, b_proj, gcn_w, gc
                 for u in range(2):
                     c0 = 2 * P * s
                     nc.tensor.transpose(o_t[:, s, u, :], words[:, c0 + u : c0 + 2 * P : 2], ident_f[:])
-            bank["o", j] = o_t
+            bank["o_t", j] = o_t
 
         def take_o(j):
             nc.scalar.copy(
                 out=grouped[j][:, 0 : 2 * D].bitcast(F32).rearrange("p (s i u) -> p s i u", s=2, u=2),
-                in_=bank["o", j][:].rearrange("p s u i -> p s i u"),
+                in_=bank["o_t", j][:].rearrange("p s u i -> p s i u"),
             )
 
-        def front_end(j):
-            aggregate(j)
-            take_agg(j)
-            transpose_o(j)
-            take_o(j)
+        def aggregate(j):
+            agg_t = new_bank("front", [P, 2, PACK, P], BF16, "agg_t%d" % j)
+            for s in range(2):
+                for t in range(PACK):
+                    nc.tensor.matmul(
+                        agg_t[:, s, t, :], lhsT=h_sb[j][:, s, t:D:PACK], rhs=aT_sb[:], start=True, stop=True
+                    )
+            bank["agg_t", j] = agg_t
+
+        def take_agg(j):
+            nc.scalar.copy(
+                out=grouped[j][:, 2 * D : 4 * D].rearrange("p (s i t) -> p s i t", s=2, t=PACK),
+                in_=bank["agg_t", j][:].rearrange("p s t i -> p s i t"),
+            )
 
         def quantise(j):
             nc.vector.quantize_mx(out=codes[j][:].bitcast(FP8X4), scales=scales[j][:], in_=grouped[j][:])
@@ -146,18 +139,16 @@ def tile_gatblock_pa_kernel(tc, h_norm, o_attn, a_gcn, w_proj, b_proj, gcn_w, gc
             bank[branch, b] = acc
 
         def add_bias(b):
-            product(0, b)
             nc.vector.tensor_tensor(out=result[b][:], in0=bank[0, b][:], in1=spread[:, 0:D], op=ADD)
 
         def apply_gain(b):
-            product(1, b)
             nc.vector.tensor_tensor(out=other[b][:], in0=bank[1, b][:], in1=spread[:, D : 2 * D], op=MULT)
 
         def join_and_store(b):
             nc.gpsimd.tensor_tensor(out=result[b][:], in0=result[b][:], in1=other[b][:], op=ADD)
-            store(b)
+            nc.sync.dma_start(out=out[b], in_=result[b][:])
 
-        def gcn_feature_major(j):
+        def product_feature_major(j):
             halves = [new_bank("front", [P, 2, 2 * P], F32, "g_t%d_%d" % (j, half)) for half in range(2)]
             for c in range(CHUNKS):
                 nc.tensor.matmul_mx(
@@ -169,43 +160,50 @@ def tile_gatblock_pa_kernel(tc, h_norm, o_attn, a_gcn, w_proj, b_proj, gcn_w, gc
                     start=True,
                     stop=True,
                 )
+            bank["g_t", j] = halves
+
+        def take_gcn(j):
             for c in range(CHUNKS):
                 nc.scalar.activation(
                     out=scaled_t[j][:, c, :],
-                    in_=halves[c // 2][:, c % 2, :],
+                    in_=bank["g_t", j][c // 2][:, c % 2, :],
                     func=IDENTITY,
                     bias=per_feature[:, c : c + 1],
                     scale=per_feature[:, CHUNKS + c : CHUNKS + c + 1],
                 )
 
-        def projection_out(b):
-            product(0, b)
+        def take_projection(b):
             nc.scalar.copy(out=other[b][:], in_=bank[0, b][:])
 
-        def turn_back_join_store(b):
+        def turn_back(b):
             back = new_bank("front", [P, D], F32, "back%d" % b)
             cols = slice(P * (b % 2), P * (b % 2) + P)
             for c in range(CHUNKS):
                 nc.tensor.transpose(back[:, P * c : P * c + P], scaled_t[b // 2][:, c, cols], ident_f[:])
-            nc.vector.tensor_tensor(out=result[b][:], in0=back[:], in1=other[b][:], op=ADD)
-            store(b, nc.scalar)
+            bank["back", b] = back
 
-        nc.scalar.dma_start(out=a_sb[:], in_=a_gcn)
-        load_h(0)
-        load_weight(0)
+        def add_and_store(b):
+            nc.vector.tensor_tensor(out=result[b][:], in0=bank["back", b][:], in1=other[b][:], op=ADD)
+            nc.scalar.dma_start(out=out[b], in_=result[b][:])
+
         nc.gpsimd.memset(zeros[:].bitcast(U32), 0)
         idle_ps = new_bank("front", [P, D], F32, "idle_ps")
-        for turn in range(4):
+        for turn in range(IDLE_MATMULS):
             nc.tensor.matmul(idle_ps[:], lhsT=zeros[:, 0:P], rhs=zeros[:], start=True, stop=True)
-        nc.vector.memset(rows[:], 0.0)
+        nc.scalar.dma_start(out=a_sb[:], in_=a_gcn)
+        nc.gpsimd.memset(zero[:], 0.0)
+        nc.scalar.activation(out=warm[:], in_=zero[:], func=IDENTITY)
+        make_identity(nc, ident_bf[:])
+        make_identity(nc, ident_f[:])
+
+        load_h(0)
+        load_weight(0)
+        nc.vector.memset(rows[:].bitcast(U32), 0)
+        nc.vector.memset(ones[:], 1.0)
+        nc.vector.memset(chunk_rows[:].bitcast(U32), 0)
         nc.scalar.dma_start(out=rows[0:1, 0:D], in_=b_proj.rearrange("(o n) -> o n", o=1))
         nc.scalar.dma_start(out=rows[0:1, D : 2 * D], in_=gcn_m.rearrange("(o n) -> o n", o=1))
         load_o(0)
-        nc.vector.memset(ones[:], 1.0)
-        nc.vector.memset(chunk_rows[:], 0.0)
-        make_identity(nc, ident_bf[:])
-        make_identity(nc, ident_f[:])
-        nc.scalar.activation(out=warm[:], in_=ident_f[:, 0:1], func=IDENTITY)
         load_h(1)
         load_o(1)
         load_weight(1)
@@ -224,54 +222,81 @@ def tile_gatblock_pa_kernel(tc, h_norm, o_attn, a_gcn, w_proj, b_proj, gcn_w, gc
         quantise_weight(0)
         transpose_o(0)
         take_o(0)
-        aggregate(1)
         spread_ps = new_bank("product", [P, 2 * D], BF16, "spread_ps")
         for half in range(2):
             cols = slice(D * half, D * half + D)
             nc.tensor.matmul(spread_ps[:, cols], lhsT=ones[:], rhs=rows[:, cols], start=True, stop=True)
         nc.scalar.copy(out=spread[:], in_=spread_ps[:])
+        quantise(0)
         transpose_o(1)
         take_o(1)
-        quantise(0)
-        regroup(nc.vector.tensor_copy, 1, SCALAR_COLS, D)
+        aggregate(1)
+        product(0, 0)
         regroup(nc.scalar.copy, 1, 0, SCALAR_COLS)
+        regroup(nc.vector.tensor_copy, 1, SCALAR_COLS, D)
         add_bias(0)
         take_agg(1)
         quantise_weight(1)
-        add_bias(1)
-        aggregate(2)
-        take_agg(2)
-        transpose_o(2)
         quantise(1)
+        aggregate(2)
+        transpose_o(2)
+        product(0, 1)
+        product(1, 0)
+        take_agg(2)
         take_o(2)
-        for b in (0, 1):
-            apply_gain(b)
-            join_and_store(b)
-
-        def finish(b):
-            add_bias(b)
-            apply_gain(b)
-            join_and_store(b)
+        add_bias(1)
+        apply_gain(0)
+        join_and_store(0)
 
         for t in range(2, PAIRS - 1):
-            front_end(t + 1)
+            aggregate(t + 1)
+            transpose_o(t + 1)
+            take_agg(t + 1)
+            take_o(t + 1)
+            product(0, t)
+            product(1, t - 1)
             quantise(t)
-            finish(t)
+            add_bias(t)
+            apply_gain(t - 1)
+            join_and_store(t - 1)
 
         chunk_cols = new_bank("front", [P, P], BF16, "chunk_cols")
         nc.tensor.transpose(chunk_cols[:], chunk_rows[:], ident_bf[:])
         nc.scalar.copy(out=per_feature[:], in_=chunk_cols[:, 0 : 2 * CHUNKS])
-        gcn_feature_major(4)
+        product_feature_major(4)
+        take_gcn(4)
+        product(0, 5)
+        product(1, 4)
         quantise(5)
-        projection_out(8)
         add_bias(5)
-        projection_out(9)
+        apply_gain(4)
+        join_and_store(4)
+        product(0, 8)
+        product(1, 5)
+        take_projection(8)
+        product_feature_major(5)
+        product(0, 9)
+        product(0, 6)
+        take_projection(9)
+        take_gcn(5)
         apply_gain(5)
         join_and_store(5)
-        gcn_feature_major(5)
-        finish(6)
-        projection_out(10)
-        projection_out(11)
-        finish(7)
-        for b in range(NODE_MAJOR, B):
-            turn_back_join_store(b)
+        turn_back(8)
+        product(1, 6)
+        add_bias(6)
+        add_and_store(8)
+        turn_back(9)
+        apply_gain(6)
+        join_and_store(6)
+        product(0, 7)
+        product(1, 7)
+        add_and_store(9)
+        add_bias(7)
+        apply_gain(7)
+        join_and_store(7)
+        for b in (10, 11):
+            product(0, b)
+            take_projection(b)
+        for b in (10, 11):
+            turn_back(b)
+            add_and_store(b)

@@ -18,7 +18,7 @@ PACK = 4
 B = 12
 PAIRS = B // 2
 CHUNKS = D // P
-NODE_MAJOR = 8
+NODE_MAJOR = 7
 FLOPS = 2 * 2 * B * P * D * D + 2 * B * P * P * D
 
 SCALAR_COLS = 128
@@ -57,7 +57,7 @@ def tile_gatblock_pa_kernel(tc, h_norm, o_attn, a_gcn, w_proj, b_proj, gcn_w, gc
         scales = [sbuf.tile([P, 4 * P], U8, name="scales%d" % j, align_bytes=64) for j in range(PAIRS)]
         result = [sbuf.tile([P, D], F32, name="result%d" % b) for b in range(B)]
         other = [sbuf.tile([P, D], F32, name="other%d" % b) for b in range(B)]
-        scaled_t = {j: sbuf.tile([P, CHUNKS, 2 * P], F32, name="scaled_t%d" % j) for j in range(NODE_MAJOR // 2, PAIRS)}
+        scaled_t = {j: sbuf.tile([P, CHUNKS, 2 * P], F32, name="scaled_t%d" % j) for j in range(3, PAIRS)}
         bank = {}
         taken = {group: 0 for group in BANKS}
 
@@ -148,25 +148,28 @@ def tile_gatblock_pa_kernel(tc, h_norm, o_attn, a_gcn, w_proj, b_proj, gcn_w, gc
             nc.gpsimd.tensor_tensor(out=result[b][:], in0=result[b][:], in1=other[b][:], op=ADD)
             nc.sync.dma_start(out=out[b], in_=result[b][:])
 
-        def product_feature_major(j):
-            halves = [new_bank("front", [P, 2, 2 * P], F32, "g_t%d_%d" % (j, half)) for half in range(2)]
+        def product_feature_major(first, count):
+            j, cols = first // 2, slice(P * (2 + first % 2), P * (2 + first % 2 + count))
+            fit = CHUNKS // count
+            banks = [new_bank("front", [P, fit, P * count], F32, "g_t%d_%d" % (first, i)) for i in range(count)]
             for c in range(CHUNKS):
                 nc.tensor.matmul_mx(
-                    out=halves[c // 2][:, c % 2, :],
+                    out=banks[c // fit][:, c % fit, :],
                     lhsT=w_codes[1][:, P * c : P * c + P].bitcast(FP8X4),
                     lhsT_scale=w_scales[1][:, P * c : P * c + P],
-                    rhs=codes[j][:, 2 * P : 4 * P].bitcast(FP8X4),
-                    rhs_scale=scales[j][:, 2 * P : 4 * P],
+                    rhs=codes[j][:, cols].bitcast(FP8X4),
+                    rhs_scale=scales[j][:, cols],
                     start=True,
                     stop=True,
                 )
-            bank["g_t", j] = halves
+            bank["g_t", first] = banks
 
-        def take_gcn(j):
+        def take_gcn(first, count):
+            fit, c0 = CHUNKS // count, P * (first % 2)
             for c in range(CHUNKS):
                 nc.scalar.activation(
-                    out=scaled_t[j][:, c, :],
-                    in_=bank["g_t", j][c // 2][:, c % 2, :],
+                    out=scaled_t[first // 2][:, c, c0 : c0 + P * count],
+                    in_=bank["g_t", first][c // fit][:, c % fit, :],
                     func=IDENTITY,
                     bias=per_feature[:, c : c + 1],
                     scale=per_feature[:, CHUNKS + c : CHUNKS + c + 1],
@@ -184,7 +187,7 @@ def tile_gatblock_pa_kernel(tc, h_norm, o_attn, a_gcn, w_proj, b_proj, gcn_w, gc
 
         def add_and_store(b):
             nc.vector.tensor_tensor(out=result[b][:], in0=bank["back", b][:], in1=other[b][:], op=ADD)
-            nc.scalar.dma_start(out=out[b], in_=result[b][:])
+            (nc.sync if b < 10 else nc.scalar).dma_start(out=out[b], in_=result[b][:])
 
         nc.gpsimd.memset(zeros[:].bitcast(U32), 0)
         idle_ps = new_bank("front", [P, D], F32, "idle_ps")
@@ -263,40 +266,43 @@ def tile_gatblock_pa_kernel(tc, h_norm, o_attn, a_gcn, w_proj, b_proj, gcn_w, gc
         chunk_cols = new_bank("front", [P, P], BF16, "chunk_cols")
         nc.tensor.transpose(chunk_cols[:], chunk_rows[:], ident_bf[:])
         nc.scalar.copy(out=per_feature[:], in_=chunk_cols[:, 0 : 2 * CHUNKS])
-        product_feature_major(4)
-        take_gcn(4)
+        product_feature_major(8, 2)
+        take_gcn(8, 2)
         product(0, 5)
         product(1, 4)
         quantise(5)
         add_bias(5)
         apply_gain(4)
         join_and_store(4)
+        product_feature_major(7, 1)
         product(0, 8)
         product(1, 5)
         take_projection(8)
-        product_feature_major(5)
-        product(0, 9)
+        take_gcn(7, 1)
+        product_feature_major(10, 2)
+        product(0, 7)
         product(0, 6)
-        take_projection(9)
-        take_gcn(5)
+        take_projection(7)
         apply_gain(5)
-        join_and_store(5)
+        product(0, 9)
+        take_gcn(10, 2)
         turn_back(8)
         product(1, 6)
         add_bias(6)
         add_and_store(8)
-        turn_back(9)
+        join_and_store(5)
+        turn_back(7)
         apply_gain(6)
+        take_projection(9)
+        add_and_store(7)
         join_and_store(6)
-        product(0, 7)
-        product(1, 7)
+        product(0, 10)
+        take_projection(10)
+        turn_back(9)
+        product(0, 11)
+        take_projection(11)
         add_and_store(9)
-        add_bias(7)
-        apply_gain(7)
-        join_and_store(7)
-        for b in (10, 11):
-            product(0, b)
-            take_projection(b)
-        for b in (10, 11):
-            turn_back(b)
-            add_and_store(b)
+        turn_back(10)
+        add_and_store(10)
+        turn_back(11)
+        add_and_store(11)

@@ -21,7 +21,7 @@ CHUNKS = D // P
 NODE_MAJOR = 7
 FLOPS = 2 * 2 * B * P * D * D + 2 * B * P * P * D
 
-SCALAR_COLS = 128
+GPSIMD_COLS = 128
 IDLE_MATMULS = 4
 BANKS = {"front": 4, "product": 4}
 
@@ -83,6 +83,9 @@ def tile_gatblock_pa_kernel(tc, h_norm, o_attn, a_gcn, w_proj, b_proj, gcn_w, gc
                 out=w_grouped[w][:, c0:c1, :].rearrange("p (c i) t -> p c t i", i=4),
                 in_=w_raw[w][:, :, c0:c1].rearrange("p t (c i) -> p c t i", i=4),
             )
+
+        def tensor_scalar_copy(out, in_):
+            nc.gpsimd.tensor_scalar(out=out, in0=in_, scalar1=1.0, scalar2=0.0, op0=MULT, op1=ADD)
 
         def quantise_weight(w):
             nc.vector.quantize_mx(
@@ -235,8 +238,8 @@ def tile_gatblock_pa_kernel(tc, h_norm, o_attn, a_gcn, w_proj, b_proj, gcn_w, gc
         take_o(1)
         aggregate(1)
         product(0, 0)
-        regroup(nc.scalar.copy, 1, 0, SCALAR_COLS)
-        regroup(nc.vector.tensor_copy, 1, SCALAR_COLS, D)
+        regroup(nc.vector.tensor_copy, 1, GPSIMD_COLS, D)
+        regroup(tensor_scalar_copy, 1, 0, GPSIMD_COLS)
         add_bias(0)
         take_agg(1)
         quantise_weight(1)

from contextlib import ExitStack

import concourse.mybir as mybir
from concourse.masks import make_identity

FP8X4 = mybir.dt.float8_e4m3fn_x4
BF16 = mybir.dt.bfloat16
F32 = mybir.dt.float32
U32 = mybir.dt.uint32
U8 = mybir.dt.uint8
ADD = mybir.AluOpType.add
MULT = mybir.AluOpType.mult
IDENTITY = mybir.ActivationFunctionType.Identity

P = 128
D = 512
PACK = 4
B = 12
PAIRS = B // 2
CHUNKS = D // P
NODE_MAJOR = 7
FLOPS = 2 * 2 * B * P * D * D + 2 * B * P * P * D

GPSIMD_COLS = 128
IDLE_MATMULS = 4
BANKS = {"front": 4, "product": 4}


def tile_gatblock_pa_kernel(tc, h_norm, o_attn, a_gcn, w_proj, b_proj, gcn_w, gcn_m, out):
    nc = tc.nc
    with ExitStack() as ctx:
        sbuf = ctx.enter_context(tc.tile_pool(name="sbuf", bufs=1))
        psum = ctx.enter_context(tc.psum_pool(name="psum", bufs=1))
        ctx.enter_context(tc.manual_schedule())

        ident_f = sbuf.tile([P, P], F32, name="ident_f")
        ident_bf = sbuf.tile([P, P], BF16, name="ident_bf")
        zeros = sbuf.tile([P, D], BF16, name="zeros")
        ones = sbuf.tile([P, P], BF16, name="ones")
        rows = sbuf.tile([P, 2 * D], BF16, name="rows")
        spread = sbuf.tile([P, 2 * D], BF16, name="spread")
        chunk_rows = sbuf.tile([P, P], BF16, name="chunk_rows")
        per_feature = sbuf.tile([P, 2 * CHUNKS], F32, name="per_feature")
        zero = sbuf.tile([P, 1], F32, name="zero")
        warm = sbuf.tile([P, 1], F32, name="warm")
        a_sb = sbuf.tile([P, P], BF16, name="a_sb")
        aT_sb = sbuf.tile([P, P], BF16, name="aT_sb")
        w_dram = (w_proj, gcn_w)
        w_raw = [sbuf.tile([P, PACK, D], BF16, name="w_raw%d" % w) for w in range(2)]
        w_grouped = [sbuf.tile([P, D, PACK], BF16, name="w_grouped%d" % w, align_bytes=64) for w in range(2)]
        w_codes = [sbuf.tile([P, D], U32, name="w_codes%d" % w, align_bytes=64) for w in range(2)]
        w_scales = [sbuf.tile([P, D], U8, name="w_scales%d" % w, align_bytes=64) for w in range(2)]
        o_sb = [sbuf.tile([P, 2 * D], BF16, name="o_sb%d" % j) for j in range(PAIRS)]
        h_sb = [sbuf.tile([P, 2, D], BF16, name="h_sb%d" % j) for j in range(PAIRS)]
        grouped = [sbuf.tile([P, 4 * D], BF16, name="grouped%d" % j, align_bytes=64) for j in range(PAIRS)]
        codes = [sbuf.tile([P, 4 * P], U32, name="codes%d" % j, align_bytes=64) for j in range(PAIRS)]
        scales = [sbuf.tile([P, 4 * P], U8, name="scales%d" % j, align_bytes=64) for j in range(PAIRS)]
        result = [sbuf.tile([P, D], F32, name="result%d" % b) for b in range(B)]
        other = [sbuf.tile([P, D], F32, name="other%d" % b) for b in range(B)]
        scaled_t = {j: sbuf.tile([P, CHUNKS, 2 * P], F32, name="scaled_t%d" % j) for j in range(3, PAIRS)}
        bank = {}
        taken = {group: 0 for group in BANKS}

        def new_bank(group, shape, dtype, name):
            tag = "%s%d" % (group, taken[group] % BANKS[group])
            taken[group] = taken[group] + 1
            return psum.tile(shape, dtype, name=name, tag=tag)

        def load_weight(w):
            nc.sync.dma_start(out=w_raw[w][:], in_=w_dram[w].rearrange("(p t) c -> p t c", t=PACK))

        def load_h(j):
            nc.sync.dma_start(out=h_sb[j][:], in_=h_norm[2 * j : 2 * j + 2].rearrange("s n d -> n s d"))

        def load_o(j):
            nc.sync.dma_start(
                out=o_sb[j][:].rearrange("p (s d) -> p s d", s=2),
                in_=o_attn[2 * j : 2 * j + 2].rearrange("s n d -> n s d"),
            )

        def regroup(copy, w, c0, c1):
            copy(
                out=w_grouped[w][:, c0:c1, :].rearrange("p (c i) t -> p c t i", i=4),
                in_=w_raw[w][:, :, c0:c1].rearrange("p t (c i) -> p c t i", i=4),
            )

        def tensor_scalar_copy(out, in_):
            nc.gpsimd.tensor_scalar(out=out, in0=in_, scalar1=1.0, scalar2=0.0, op0=MULT, op1=ADD)

        def quantise_weight(w):
            nc.vector.quantize_mx(
                out=w_codes[w][:].bitcast(FP8X4),
                scales=w_scales[w][:],
                in_=w_grouped[w][:].rearrange("p c t -> p (c t)"),
            )

        def transpose_o(j):
            o_t = new_bank("front", [P, 2, 2, P], F32, "o_t%d" % j)
            words = o_sb[j][:].bitcast(F32)
            for s in range(2):
                for u in range(2):
                    c0 = 2 * P * s
                    nc.tensor.transpose(o_t[:, s, u, :], words[:, c0 + u : c0 + 2 * P : 2], ident_f[:])
            bank["o_t", j] = o_t

        def take_o(j):
            nc.scalar.copy(
                out=grouped[j][:, 0 : 2 * D].bitcast(F32).rearrange("p (s i u) -> p s i u", s=2, u=2),
                in_=bank["o_t", j][:].rearrange("p s u i -> p s i u"),
            )

        def aggregate(j):
            agg_t = new_bank("front", [P, 2, PACK, P], BF16, "agg_t%d" % j)
            for s in range(2):
                for t in range(PACK):
                    nc.tensor.matmul(
                        agg_t[:, s, t, :], lhsT=h_sb[j][:, s, t:D:PACK], rhs=aT_sb[:], start=True, stop=True
                    )
            bank["agg_t", j] = agg_t

        def take_agg(j):
            nc.scalar.copy(
                out=grouped[j][:, 2 * D : 4 * D].rearrange("p (s i t) -> p s i t", s=2, t=PACK),
                in_=bank["agg_t", j][:].rearrange("p s t i -> p s i t"),
            )

        def quantise(j):
            nc.vector.quantize_mx(out=codes[j][:].bitcast(FP8X4), scales=scales[j][:], in_=grouped[j][:])

        def product(branch, b):
            j, c0 = b // 2, P * (2 * branch + b % 2)
            acc = new_bank("product", [P, D], F32, "acc%d_%d" % (branch, b))
            nc.tensor.matmul_mx(
                out=acc[:],
                lhsT=codes[j][:, c0 : c0 + P].bitcast(FP8X4),
                lhsT_scale=scales[j][:, c0 : c0 + P],
                rhs=w_codes[branch][:].bitcast(FP8X4),
                rhs_scale=w_scales[branch][:],
                start=True,
                stop=True,
            )
            bank[branch, b] = acc

        def add_bias(b):
            nc.vector.tensor_tensor(out=result[b][:], in0=bank[0, b][:], in1=spread[:, 0:D], op=ADD)

        def apply_gain(b):
            nc.vector.tensor_tensor(out=other[b][:], in0=bank[1, b][:], in1=spread[:, D : 2 * D], op=MULT)

        def join_and_store(b):
            nc.gpsimd.tensor_tensor(out=result[b][:], in0=result[b][:], in1=other[b][:], op=ADD)
            nc.sync.dma_start(out=out[b], in_=result[b][:])

        def product_feature_major(first, count):
            j, cols = first // 2, slice(P * (2 + first % 2), P * (2 + first % 2 + count))
            fit = CHUNKS // count
            banks = [new_bank("front", [P, fit, P * count], F32, "g_t%d_%d" % (first, i)) for i in range(count)]
            for c in range(CHUNKS):
                nc.tensor.matmul_mx(
                    out=banks[c // fit][:, c % fit, :],
                    lhsT=w_codes[1][:, P * c : P * c + P].bitcast(FP8X4),
                    lhsT_scale=w_scales[1][:, P * c : P * c + P],
                    rhs=codes[j][:, cols].bitcast(FP8X4),
                    rhs_scale=scales[j][:, cols],
                    start=True,
                    stop=True,
                )
            bank["g_t", first] = banks

        def take_gcn(first, count):
            fit, c0 = CHUNKS // count, P * (first % 2)
            for c in range(CHUNKS):
                nc.scalar.activation(
                    out=scaled_t[first // 2][:, c, c0 : c0 + P * count],
                    in_=bank["g_t", first][c // fit][:, c % fit, :],
                    func=IDENTITY,
                    bias=per_feature[:, c : c + 1],
                    scale=per_feature[:, CHUNKS + c : CHUNKS + c + 1],
                )

        def take_projection(b):
            nc.scalar.copy(out=other[b][:], in_=bank[0, b][:])

        def turn_back(b):
            back = new_bank("front", [P, D], F32, "back%d" % b)
            cols = slice(P * (b % 2), P * (b % 2) + P)
            for c in range(CHUNKS):
                nc.tensor.transpose(back[:, P * c : P * c + P], scaled_t[b // 2][:, c, cols], ident_f[:])
            bank["back", b] = back

        def add_and_store(b):
            nc.vector.tensor_tensor(out=result[b][:], in0=bank["back", b][:], in1=other[b][:], op=ADD)
            (nc.sync if b < 10 else nc.scalar).dma_start(out=out[b], in_=result[b][:])

        nc.gpsimd.memset(zeros[:].bitcast(U32), 0)
        idle_ps = new_bank("front", [P, D], F32, "idle_ps")
        for turn in range(IDLE_MATMULS):
            nc.tensor.matmul(idle_ps[:], lhsT=zeros[:, 0:P], rhs=zeros[:], start=True, stop=True)
        nc.scalar.dma_start(out=a_sb[:], in_=a_gcn)
        nc.gpsimd.memset(zero[:], 0.0)
        nc.scalar.activation(out=warm[:], in_=zero[:], func=IDENTITY)
        make_identity(nc, ident_bf[:])
        make_identity(nc, ident_f[:])

        load_h(0)
        load_weight(0)
        nc.vector.memset(rows[:].bitcast(U32), 0)
        nc.vector.memset(ones[:], 1.0)
        nc.vector.memset(chunk_rows[:].bitcast(U32), 0)
        nc.scalar.dma_start(out=rows[0:1, 0:D], in_=b_proj.rearrange("(o n) -> o n", o=1))
        nc.scalar.dma_start(out=rows[0:1, D : 2 * D], in_=gcn_m.rearrange("(o n) -> o n", o=1))
        load_o(0)
        load_h(1)
        load_o(1)
        load_weight(1)
        for j in range(2, PAIRS):
            load_h(j)
            load_o(j)
        nc.sync.dma_start(out=chunk_rows[0:CHUNKS, :], in_=b_proj.rearrange("(c p) -> c p", p=P))
        nc.sync.dma_start(out=chunk_rows[CHUNKS : 2 * CHUNKS, :], in_=gcn_m.rearrange("(c p) -> c p", p=P))

        a_t = new_bank("front", [P, P], BF16, "a_t")
        nc.tensor.transpose(a_t[:], a_sb[:], ident_bf[:])
        nc.scalar.copy(out=aT_sb[:], in_=a_t[:])
        aggregate(0)
        take_agg(0)
        regroup(nc.vector.tensor_copy, 0, 0, D)
        quantise_weight(0)
        transpose_o(0)
        take_o(0)
        spread_ps = new_bank("product", [P, 2 * D], BF16, "spread_ps")
        for half in range(2):
            cols = slice(D * half, D * half + D)
            nc.tensor.matmul(spread_ps[:, cols], lhsT=ones[:], rhs=rows[:, cols], start=True, stop=True)
        nc.scalar.copy(out=spread[:], in_=spread_ps[:])
        quantise(0)
        transpose_o(1)
        take_o(1)
        aggregate(1)
        product(0, 0)
        regroup(nc.vector.tensor_copy, 1, GPSIMD_COLS, D)
        regroup(tensor_scalar_copy, 1, 0, GPSIMD_COLS)
        add_bias(0)
        take_agg(1)
        quantise_weight(1)
        quantise(1)
        aggregate(2)
        transpose_o(2)
        product(0, 1)
        product(1, 0)
        take_agg(2)
        take_o(2)
        add_bias(1)
        apply_gain(0)
        join_and_store(0)

        for t in range(2, PAIRS - 1):
            aggregate(t + 1)
            transpose_o(t + 1)
            take_agg(t + 1)
            take_o(t + 1)
            product(0, t)
            product(1, t - 1)
            quantise(t)
            add_bias(t)
            apply_gain(t - 1)
            join_and_store(t - 1)

        chunk_cols = new_bank("front", [P, P], BF16, "chunk_cols")
        nc.tensor.transpose(chunk_cols[:], chunk_rows[:], ident_bf[:])
        nc.scalar.copy(out=per_feature[:], in_=chunk_cols[:, 0 : 2 * CHUNKS])
        product_feature_major(8, 2)
        take_gcn(8, 2)
        product(0, 5)
        product(1, 4)
        quantise(5)
        add_bias(5)
        apply_gain(4)
        join_and_store(4)
        product_feature_major(7, 1)
        product(0, 8)
        product(1, 5)
        take_projection(8)
        take_gcn(7, 1)
        product_feature_major(10, 2)
        product(0, 7)
        product(0, 6)
        take_projection(7)
        apply_gain(5)
        product(0, 9)
        take_gcn(10, 2)
        turn_back(8)
        product(1, 6)
        add_bias(6)
        add_and_store(8)
        join_and_store(5)
        turn_back(7)
        apply_gain(6)
        take_projection(9)
        add_and_store(7)
        join_and_store(6)
        product(0, 10)
        take_projection(10)
        turn_back(9)
        product(0, 11)
        take_projection(11)
        add_and_store(9)
        turn_back(10)
        add_and_store(10)
        turn_back(11)
        add_and_store(11)
